import numpy as np
import ml_dtypes


def mxq(x, axis, fmt="e4m3"):
    dtype, down = {"e4m3": (ml_dtypes.float8_e4m3fn, 7), "e5m2": (ml_dtypes.float8_e5m2, 14)}[fmt]
    v = np.moveaxis(np.asarray(x, np.float32).astype(ml_dtypes.bfloat16).astype(np.float64), axis, -1)
    blocks = v.reshape(v.shape[:-1] + (-1, 32))
    amax = np.abs(blocks).max(-1, keepdims=True)
    byte = np.maximum(np.where(amax > 0, np.frexp(amax)[1] - 1 + 127, 0) - down, 1)
    scale = np.exp2(byte - 127.0)
    codes = (blocks / scale).astype(np.float32).astype(dtype).astype(np.float64)
    return np.moveaxis((codes * scale).reshape(v.shape), -1, axis)


WIDE = False


def mx_kscale(k):
    if not WIDE:
        return np.ones(k)
    levels = np.array([10, -10, 5, -5, 0])
    a = np.random.permutation(np.resize(levels, k // 512 * 4)).reshape(k // 512, 4)
    idx = np.arange(k)
    return np.exp2(a[idx // 512, idx % 128 // 32])


BF16 = ml_dtypes.bfloat16


def bf(x):
    return np.asarray(x, np.float32).astype(BF16)


def f64(x):
    return np.asarray(x).astype(np.float64)


B, S, D = 32, 256, 512
NB = 2
W = 2 * NB + 1
LN_EPS = 1e-5


def setup_inputs():
    s = mx_kscale(D)
    u = s / s.max()
    pos = np.arange(S)[:, None] + np.arange(W)[None, :] - NB
    e = np.exp(np.random.standard_normal((B, S, W))) * ((pos >= 0) & (pos < S))
    return {"x": bf(np.random.standard_normal((B, S, D)) * u),
            "Wv": bf(np.random.standard_normal((D, D)) / np.sqrt(D) / u[None, :]),
            "bv": bf(0.2 + 0.2 * np.random.standard_normal(D)),
            "attn_band": bf(e / e.sum(-1, keepdims=True)),
            "gamma": bf(1.0 + 0.1 * np.random.standard_normal(D)),
            "beta": bf(0.2 * np.random.standard_normal(D))}


def reference(x, Wv, bv, attn_band, gamma, beta):
    xf, a = f64(x), f64(attn_band)
    v = (mxq(xf, 2, "e4m3") @ mxq(f64(Wv), 1, "e4m3").T) + f64(bv)
    mix = np.zeros_like(xf)
    for j in range(W):
        o = j - NB
        lo, hi = max(0, -o), S - max(0, o)
        mix[:, lo:hi] += a[:, lo:hi, j:j + 1] * v[:, lo + o:hi + o]
    out = mix + xf
    mu = out.mean(-1, keepdims=True)
    var = out.var(-1, keepdims=True)
    return (out - mu) / np.sqrt(var + LN_EPS) * f64(gamma) + f64(beta)

@@ -1,0 +1,231 @@
+from contextlib import ExitStack
+
+import concourse.mybir as mybir
+from concourse.masks import make_identity
+
+F32 = mybir.dt.float32
+BF16 = mybir.dt.bfloat16
+U32 = mybir.dt.uint32
+U8 = mybir.dt.uint8
+I32 = mybir.dt.int32
+FP8X4 = mybir.dt.float8_e4m3fn_x4
+ALU = mybir.AluOpType
+ACT = mybir.ActivationFunctionType
+AX = mybir.AxisListType
+
+P = 128
+D = 512
+ROWS = 8192
+RUN = ROWS // P
+TAPS = 5
+NB = 2
+GRP = 4
+EPS = 1e-5
+CHUNK = 8
+
+FLOPS = 2 * ROWS * D * D + 2 * ROWS * TAPS * D
+
+
+def tile_crosssliceattention_pb_t_kernel(tc, x, Wv, bv, attn_band, gamma, beta, out):
+    nc = tc.nc
+    xf = x.flatten_outer_dims()
+    x_rows = xf.rearrange("(p t) d -> p t d", t=RUN)
+    o_rows = out.flatten_outer_dims().rearrange("(p t) d -> p t d", t=RUN)
+
+    with ExitStack() as ctx:
+        const = ctx.enter_context(tc.tile_pool(name="const", bufs=1))
+        grp_pool = ctx.enter_context(tc.tile_pool(name="grp", bufs=2))
+        acc_pool = ctx.enter_context(tc.tile_pool(name="accp", bufs=14))
+        junk_pool = ctx.enter_context(tc.tile_pool(name="junkp", bufs=2))
+        stat_pool = ctx.enter_context(tc.tile_pool(name="statp", bufs=3))
+        big_pool = ctx.enter_context(tc.tile_pool(name="bigp", bufs=2))
+        out_pool = ctx.enter_context(tc.tile_pool(name="outp", bufs=3))
+        psx = ctx.enter_context(tc.psum_pool(name="psx", bufs=2))
+        psv = ctx.enter_context(tc.psum_pool(name="psv", bufs=2))
+        psf = ctx.enter_context(tc.psum_pool(name="psf", bufs=2))
+        psb = ctx.enter_context(tc.psum_pool(name="psb", bufs=2))
+
+        w_raw = const.tile([P, GRP, D], BF16, name="w_raw")
+        nc.sync.dma_start(out=w_raw[:], in_=Wv.rearrange("(c p) k -> p c k", p=P))
+        halo = const.tile([P, 2 * NB, D], BF16, name="halo")
+        nc.vector.memset(halo[:].bitcast(I32), 0)
+        lo_view = xf[RUN - NB : RUN - NB + RUN * (P - 1), :].rearrange("(p t) d -> p t d", t=RUN)
+        hi_view = xf[RUN:ROWS, :].rearrange("(p t) d -> p t d", t=RUN)
+        nc.sync.dma_start(out=halo[1:113, 0:NB, :], in_=lo_view[0:112, 0:NB, :])
+        nc.sync.dma_start(out=halo[113:128, 0:NB, :], in_=lo_view[112:127, 0:NB, :])
+        xc = []
+        for k in range(RUN // CHUNK):
+            t = const.tile([P, CHUNK, D], BF16, name="xc%d" % k)
+            nc.sync.dma_start(out=t[:], in_=x_rows[:, k * CHUNK : (k + 1) * CHUNK, :])
+            xc.append(t)
+        nc.sync.dma_start(out=halo[0:112, NB : 2 * NB, :], in_=hi_view[0:112, 0:NB, :])
+        nc.sync.dma_start(out=halo[112:127, NB : 2 * NB, :], in_=hi_view[112:127, 0:NB, :])
+
+        a_bf = const.tile([P, RUN * TAPS], BF16, name="a_bf")
+        nc.scalar.dma_start(
+            out=a_bf[:], in_=attn_band.flatten_outer_dims().rearrange("(p t) j -> p (t j)", t=RUN)
+        )
+        bvb = const.tile([P, D], BF16, name="bvb")
+        nc.scalar.dma_start(out=bvb[:], in_=bv.partition_broadcast(P))
+        gbrow = const.tile([P, P], BF16, name="gbrow")
+        nc.vector.memset(gbrow[:], 0.0)
+        nc.scalar.dma_start(out=gbrow[0:4, :], in_=gamma.rearrange("(c p) -> c p", p=P))
+        nc.scalar.dma_start(out=gbrow[4:8, :], in_=beta.rearrange("(c p) -> c p", p=P))
+
+        ident_f = const.tile([P, P], F32, name="ident_f")
+        make_identity(nc, ident_f[:])
+        ident_b = const.tile([P, P], BF16, name="ident_b")
+        make_identity(nc, ident_b[:])
+
+        mhalf = const.tile([P, GRP], F32, name="mhalf")
+        nc.vector.memset(mhalf[:], -0.5)
+
+        def x_tile(i):
+            if i < 0:
+                return halo[:, i + NB, :]
+            if i >= RUN:
+                return halo[:, i - RUN + NB, :]
+            return xc[i // CHUNK][:, i % CHUNK, :]
+
+        a_f = const.tile([P, RUN, TAPS], F32, name="a_f")
+        nc.vector.tensor_copy(out=a_f[:].rearrange("p t j -> p (t j)"), in_=a_bf[:])
+        csum = const.tile([P, RUN], F32, name="csum")
+        nc.vector.reduce_sum(out=csum[:], in_=a_f[:], axis=AX.X)
+
+        gps = psx.tile([P, P], BF16, name="gps", tag="xt")
+        nc.tensor.transpose(out=gps[:], in_=gbrow[:], identity=ident_b[:])
+        gb = const.tile([P, 8], F32, name="gb")
+        nc.vector.tensor_copy(out=gb[:], in_=gps[:, 0:8])
+
+        def quantise_group(srcs, codes, scales):
+            grouped = grp_pool.tile([P, GRP * D], BF16, name="grouped", align_bytes=64)
+            g32 = grouped[:].bitcast(F32).rearrange("p (a t u) -> p a t u", a=GRP, u=2)
+            for h in range(2):
+                xt = psx.tile([P, 2, 2, P], F32, name="xt", tag="xt")
+                for a in range(2):
+                    w32 = srcs[2 * h + a].bitcast(F32)
+                    for u in range(2):
+                        nc.tensor.transpose(
+                            out=xt[:, a, u, :], in_=w32[:, u * P : (u + 1) * P], identity=ident_f[:]
+                        )
+                nc.scalar.copy(
+                    out=g32[:, 2 * h : 2 * h + 2, :, :], in_=xt[:].rearrange("p a u t -> p a t u")
+                )
+            nc.vector.quantize_mx(out=codes.bitcast(FP8X4), scales=scales, in_=grouped[:])
+
+        w_codes = const.tile([P, D], U32, name="w_codes", align_bytes=64)
+        w_scales = const.tile([P, D], U8, name="w_scales", align_bytes=64)
+        quantise_group([w_raw[:, c, :] for c in range(GRP)], w_codes[:], w_scales[:])
+
+        n_in_groups = (RUN + 2 * NB) // GRP
+        n_out_groups = RUN // GRP
+
+        def quantise_x(gi):
+            codes = grp_pool.tile([P, D], U32, name="codes", align_bytes=64)
+            scales = grp_pool.tile([P, D], U8, name="scales", align_bytes=64)
+            quantise_group([x_tile(GRP * gi - NB + a) for a in range(GRP)], codes[:], scales[:])
+            return codes, scales
+
+        acc = {}
+        sums = {}
+
+        def init_acc(g):
+            sums[g] = stat_pool.tile([P, GRP], F32, name="sums")
+            for a in range(GRP):
+                m = GRP * g + a
+                t = acc_pool.tile([P, D], F32, name="acc")
+                nc.scalar.activation(out=t[:], in_=bvb[:], func=ACT.Copy, scale=csum[:, m : m + 1])
+                nc.gpsimd.tensor_tensor(out=t[:], in0=t[:], in1=x_tile(m), op=ALU.add)
+                acc[m] = t
+
+        def finish(g):
+            negmu = stat_pool.tile([P, GRP], F32, name="negmu")
+            nc.scalar.mul(out=negmu[:], in_=sums[g][:], mul=-1.0 / D)
+            ssq = stat_pool.tile([P, GRP], F32, name="ssq")
+            for a in range(GRP):
+                junk = junk_pool.tile([P, D], BF16, name="junk")
+                nc.scalar.activation(
+                    out=junk[:],
+                    in_=acc[GRP * g + a][:],
+                    func=ACT.Square,
+                    bias=negmu[:, a : a + 1],
+                    scale=1.0,
+                    accum_out=ssq[:, a : a + 1],
+                )
+            var = stat_pool.tile([P, GRP], F32, name="var")
+            nc.gpsimd.tensor_scalar(
+                out=var[:], in0=ssq[:], scalar1=1.0 / D, scalar2=EPS, op0=ALU.mult, op1=ALU.add
+            )
+            rstd = stat_pool.tile([P, GRP], F32, name="rstd")
+            nc.gpsimd.tensor_tensor(out=rstd[:], in0=var[:], in1=mhalf[:], op=ALU.pow)
+            nrm = big_pool.tile([P, GRP, D], F32, name="nrm")
+            for a in range(GRP):
+                nc.gpsimd.tensor_scalar(
+                    out=nrm[:, a, :],
+                    in0=acc[GRP * g + a][:],
+                    scalar1=negmu[:, a : a + 1],
+                    scalar2=rstd[:, a : a + 1],
+                    op0=ALU.add,
+                    op1=ALU.mult,
+                )
+            y_t = big_pool.tile([P, GRP, GRP * P], F32, name="y_t")
+            for c in range(GRP):
+                f_ps = psf.tile([P, GRP * P], F32, name="f_ps")
+                for a in range(GRP):
+                    nc.tensor.transpose(
+                        out=f_ps[:, a * P : (a + 1) * P],
+                        in_=nrm[:, a, c * P : (c + 1) * P],
+                        identity=ident_f[:],
+                    )
+                nc.scalar.activation(
+                    out=y_t[:, c, :],
+                    in_=f_ps[:],
+                    func=ACT.Identity,
+                    scale=gb[:, c : c + 1],
+                    bias=gb[:, 4 + c : 5 + c],
+                )
+            o_sb = out_pool.tile([P, GRP, D], F32, name="o_sb")
+            for a in range(GRP):
+                b_ps = psb.tile([P, D], F32, name="b_ps")
+                for c in range(GRP):
+                    nc.tensor.transpose(
+                        out=b_ps[:, c * P : (c + 1) * P],
+                        in_=y_t[:, c, a * P : (a + 1) * P],
+                        identity=ident_f[:],
+                    )
+                nc.scalar.copy(out=o_sb[:, a, :], in_=b_ps[:])
+            nc.sync.dma_start(out=o_rows[:, GRP * g : GRP * (g + 1), :], in_=o_sb[:])
+
+        nxt = quantise_x(0)
+        for gi in range(n_in_groups):
+            codes, scales = nxt
+            if gi < n_out_groups:
+                init_acc(gi)
+            if gi + 1 < n_in_groups:
+                nxt = quantise_x(gi + 1)
+            for a in range(GRP):
+                i = GRP * gi - NB + a
+                v_ps = psv.tile([P, D], F32, name="v_ps")
+                nc.tensor.matmul_mx(
+                    out=v_ps[:],
+                    lhsT=codes[:, a * P : (a + 1) * P].bitcast(FP8X4),
+                    lhsT_scale=scales[:, a * P : (a + 1) * P],
+                    rhs=w_codes[:].bitcast(FP8X4),
+                    rhs_scale=w_scales[:],
+                    start=True,
+                    stop=True,
+                )
+                for j in range(TAPS - 1, -1, -1):
+                    m = i + NB - j
+                    if 0 <= m < RUN:
+                        nc.vector.scalar_tensor_tensor(
+                            out=acc[m][:],
+                            in0=v_ps[:],
+                            scalar=a_f[:, m, j : j + 1],
+                            in1=acc[m][:],
+                            op0=ALU.mult,
+                            op1=ALU.add,
+                            accum_out=(sums[m // GRP][:, m % GRP : m % GRP + 1] if j == TAPS - 1 else None),
+                        )
+            if gi >= 1:
+                finish(gi - 1)

@@ -35,15 +35,16 @@ def tile_crosssliceattention_pb_t_kernel(tc, x, Wv, bv, attn_band, gamma, beta, 
     with ExitStack() as ctx:
         const = ctx.enter_context(tc.tile_pool(name="const", bufs=1))
         grp_pool = ctx.enter_context(tc.tile_pool(name="grp", bufs=2))
-        acc_pool = ctx.enter_context(tc.tile_pool(name="accp", bufs=14))
+        acc_pool = ctx.enter_context(tc.tile_pool(name="accp", bufs=18))
         junk_pool = ctx.enter_context(tc.tile_pool(name="junkp", bufs=2))
-        stat_pool = ctx.enter_context(tc.tile_pool(name="statp", bufs=3))
+        stat_pool = ctx.enter_context(tc.tile_pool(name="statp", bufs=5))
         big_pool = ctx.enter_context(tc.tile_pool(name="bigp", bufs=2))
         out_pool = ctx.enter_context(tc.tile_pool(name="outp", bufs=3))
-        psx = ctx.enter_context(tc.psum_pool(name="psx", bufs=2))
-        psv = ctx.enter_context(tc.psum_pool(name="psv", bufs=2))
+        psx = ctx.enter_context(tc.psum_pool(name="psx", bufs=1))
+        psv = ctx.enter_context(tc.psum_pool(name="psv", bufs=3))
         psf = ctx.enter_context(tc.psum_pool(name="psf", bufs=2))
         psb = ctx.enter_context(tc.psum_pool(name="psb", bufs=2))
+        ctx.enter_context(tc.manual_schedule())
 
         w_raw = const.tile([P, GRP, D], BF16, name="w_raw")
         nc.sync.dma_start(out=w_raw[:], in_=Wv.rearrange("(c p) k -> p c k", p=P))
@@ -97,135 +98,222 @@ def tile_crosssliceattention_pb_t_kernel(tc, x, Wv, bv, attn_band, gamma, beta, 
         gb = const.tile([P, 8], F32, name="gb")
         nc.vector.tensor_copy(out=gb[:], in_=gps[:, 0:8])
 
-        def quantise_group(srcs, codes, scales):
-            grouped = grp_pool.tile([P, GRP * D], BF16, name="grouped", align_bytes=64)
-            g32 = grouped[:].bitcast(F32).rearrange("p (a t u) -> p a t u", a=GRP, u=2)
-            for h in range(2):
-                xt = psx.tile([P, 2, 2, P], F32, name="xt", tag="xt")
-                for a in range(2):
-                    w32 = srcs[2 * h + a].bitcast(F32)
-                    for u in range(2):
-                        nc.tensor.transpose(
-                            out=xt[:, a, u, :], in_=w32[:, u * P : (u + 1) * P], identity=ident_f[:]
-                        )
-                nc.scalar.copy(
-                    out=g32[:, 2 * h : 2 * h + 2, :, :], in_=xt[:].rearrange("p a u t -> p a t u")
-                )
-            nc.vector.quantize_mx(out=codes.bitcast(FP8X4), scales=scales, in_=grouped[:])
+        grouped = {}
+        xt_ps = {}
+
+        def turn(key, srcs, h):
+            xt = psx.tile([P, 2, 2, P], F32, name="xt", tag="xt")
+            for a in range(2):
+                w32 = srcs[2 * h + a].bitcast(F32)
+                for u in range(2):
+                    nc.tensor.transpose(
+                        out=xt[:, a, u, :], in_=w32[:, u * P : (u + 1) * P], identity=ident_f[:]
+                    )
+            xt_ps[key] = xt
+
+        def regroup(key, h):
+            if h == 0:
+                grouped[key] = grp_pool.tile([P, GRP * D], BF16, name="grouped", align_bytes=64)
+            g32 = grouped[key][:].bitcast(F32).rearrange("p (a t u) -> p a t u", a=GRP, u=2)
+            nc.scalar.copy(
+                out=g32[:, 2 * h : 2 * h + 2, :, :], in_=xt_ps[key][:].rearrange("p a u t -> p a t u")
+            )
+
+        def quantise(key, codes, scales):
+            nc.vector.quantize_mx(out=codes.bitcast(FP8X4), scales=scales, in_=grouped[key][:])
 
         w_codes = const.tile([P, D], U32, name="w_codes", align_bytes=64)
         w_scales = const.tile([P, D], U8, name="w_scales", align_bytes=64)
-        quantise_group([w_raw[:, c, :] for c in range(GRP)], w_codes[:], w_scales[:])
+        w_srcs = [w_raw[:, c, :] for c in range(GRP)]
+        for h in range(2):
+            turn("w", w_srcs, h)
+            regroup("w", h)
+        quantise("w", w_codes[:], w_scales[:])
 
-        n_in_groups = (RUN + 2 * NB) // GRP
-        n_out_groups = RUN // GRP
+        NT = RUN + 2 * NB
+        NG_IN = NT // GRP
+        NG = RUN // GRP
 
-        def quantise_x(gi):
-            codes = grp_pool.tile([P, D], U32, name="codes", align_bytes=64)
-            scales = grp_pool.tile([P, D], U8, name="scales", align_bytes=64)
-            quantise_group([x_tile(GRP * gi - NB + a) for a in range(GRP)], codes[:], scales[:])
-            return codes, scales
+        def x_srcs(g):
+            return [x_tile(GRP * g - NB + a) for a in range(GRP)]
 
+        codes = {}
+        scales = {}
+        v_ps = {}
         acc = {}
         sums = {}
+        ssq = {}
+        mu = {}
+        rstd = {}
+        nrm = {}
+        y_t = {}
+        o_sb = {}
+        f_ps = {}
+        b_ps = {}
 
-        def init_acc(g):
-            sums[g] = stat_pool.tile([P, GRP], F32, name="sums")
-            for a in range(GRP):
-                m = GRP * g + a
-                t = acc_pool.tile([P, D], F32, name="acc")
-                nc.scalar.activation(out=t[:], in_=bvb[:], func=ACT.Copy, scale=csum[:, m : m + 1])
-                nc.gpsimd.tensor_tensor(out=t[:], in0=t[:], in1=x_tile(m), op=ALU.add)
-                acc[m] = t
+        def project(k):
+            g, a = divmod(k, GRP)
+            v_ps[k] = psv.tile([P, D], F32, name="v_ps")
+            nc.tensor.matmul_mx(
+                out=v_ps[k][:],
+                lhsT=codes[g][:, a * P : (a + 1) * P].bitcast(FP8X4),
+                lhsT_scale=scales[g][:, a * P : (a + 1) * P],
+                rhs=w_codes[:].bitcast(FP8X4),
+                rhs_scale=w_scales[:],
+                start=True,
+                stop=True,
+            )
 
-        def finish(g):
-            negmu = stat_pool.tile([P, GRP], F32, name="negmu")
-            nc.scalar.mul(out=negmu[:], in_=sums[g][:], mul=-1.0 / D)
-            ssq = stat_pool.tile([P, GRP], F32, name="ssq")
-            for a in range(GRP):
-                junk = junk_pool.tile([P, D], BF16, name="junk")
-                nc.scalar.activation(
-                    out=junk[:],
-                    in_=acc[GRP * g + a][:],
-                    func=ACT.Square,
-                    bias=negmu[:, a : a + 1],
-                    scale=1.0,
-                    accum_out=ssq[:, a : a + 1],
-                )
+        def taps(k):
+            for j in range(TAPS - 1, -1, -1):
+                m = k - j
+                if 0 <= m < RUN:
+                    g, a = divmod(m, GRP)
+                    nc.vector.scalar_tensor_tensor(
+                        out=acc[m][:],
+                        in0=v_ps[k][:],
+                        scalar=a_f[:, m, j : j + 1],
+                        in1=acc[m][:],
+                        op0=ALU.mult,
+                        op1=ALU.add,
+                        accum_out=(sums[g][:, a : a + 1] if j == TAPS - 1 else None),
+                    )
+
+        def bias_part(m):
+            g, a = divmod(m, GRP)
+            if a == 0:
+                sums[g] = stat_pool.tile([P, GRP], F32, name="sums")
+                ssq[g] = stat_pool.tile([P, GRP], F32, name="ssq")
+            acc[m] = acc_pool.tile([P, D], F32, name="acc")
+            nc.scalar.activation(out=acc[m][:], in_=bvb[:], func=ACT.Copy, scale=csum[:, m : m + 1])
+
+        def residual(m):
+            nc.gpsimd.tensor_tensor(out=acc[m][:], in0=acc[m][:], in1=x_tile(m), op=ALU.add)
+
+        def squares(m):
+            g, a = divmod(m, GRP)
+            junk = junk_pool.tile([P, D], BF16, name="junk")
+            nc.scalar.activation(
+                out=junk[:],
+                in_=acc[m][:],
+                func=ACT.Square,
+                bias=sums[g][:, a : a + 1],
+                scale=-1.0 * D,
+                accum_out=ssq[g][:, a : a + 1],
+            )
+
+        def stats(g):
+            mu[g] = stat_pool.tile([P, GRP], F32, name="mu")
+            nc.gpsimd.tensor_scalar(
+                out=mu[g][:], in0=sums[g][:], scalar1=1.0 / D, scalar2=0.0, op0=ALU.mult, op1=ALU.add
+            )
             var = stat_pool.tile([P, GRP], F32, name="var")
             nc.gpsimd.tensor_scalar(
-                out=var[:], in0=ssq[:], scalar1=1.0 / D, scalar2=EPS, op0=ALU.mult, op1=ALU.add
+                out=var[:], in0=ssq[g][:], scalar1=1.0 / (D * D * D), scalar2=EPS, op0=ALU.mult, op1=ALU.add
             )
-            rstd = stat_pool.tile([P, GRP], F32, name="rstd")
-            nc.gpsimd.tensor_tensor(out=rstd[:], in0=var[:], in1=mhalf[:], op=ALU.pow)
-            nrm = big_pool.tile([P, GRP, D], F32, name="nrm")
-            for a in range(GRP):
-                nc.gpsimd.tensor_scalar(
-                    out=nrm[:, a, :],
-                    in0=acc[GRP * g + a][:],
-                    scalar1=negmu[:, a : a + 1],
-                    scalar2=rstd[:, a : a + 1],
-                    op0=ALU.add,
-                    op1=ALU.mult,
-                )
-            y_t = big_pool.tile([P, GRP, GRP * P], F32, name="y_t")
-            for c in range(GRP):
-                f_ps = psf.tile([P, GRP * P], F32, name="f_ps")
-                for a in range(GRP):
-                    nc.tensor.transpose(
-                        out=f_ps[:, a * P : (a + 1) * P],
-                        in_=nrm[:, a, c * P : (c + 1) * P],
-                        identity=ident_f[:],
-                    )
-                nc.scalar.activation(
-                    out=y_t[:, c, :],
-                    in_=f_ps[:],
-                    func=ACT.Identity,
-                    scale=gb[:, c : c + 1],
-                    bias=gb[:, 4 + c : 5 + c],
-                )
-            o_sb = out_pool.tile([P, GRP, D], F32, name="o_sb")
-            for a in range(GRP):
-                b_ps = psb.tile([P, D], F32, name="b_ps")
-                for c in range(GRP):
-                    nc.tensor.transpose(
-                        out=b_ps[:, c * P : (c + 1) * P],
-                        in_=y_t[:, c, a * P : (a + 1) * P],
-                        identity=ident_f[:],
-                    )
-                nc.scalar.copy(out=o_sb[:, a, :], in_=b_ps[:])
-            nc.sync.dma_start(out=o_rows[:, GRP * g : GRP * (g + 1), :], in_=o_sb[:])
+            rstd[g] = stat_pool.tile([P, GRP], F32, name="rstd")
+            nc.gpsimd.tensor_tensor(out=rstd[g][:], in0=var[:], in1=mhalf[:], op=ALU.pow)
+            nrm[g] = big_pool.tile([P, GRP, D], F32, name="nrm")
 
-        nxt = quantise_x(0)
-        for gi in range(n_in_groups):
-            codes, scales = nxt
-            if gi < n_out_groups:
-                init_acc(gi)
-            if gi + 1 < n_in_groups:
-                nxt = quantise_x(gi + 1)
+        def normalise(m):
+            g, a = divmod(m, GRP)
+            nc.gpsimd.tensor_scalar(
+                out=nrm[g][:, a, :],
+                in0=acc[m][:],
+                scalar1=mu[g][:, a : a + 1],
+                scalar2=rstd[g][:, a : a + 1],
+                op0=ALU.subtract,
+                op1=ALU.mult,
+            )
+
+        def to_features(g, c):
+            f_ps[c] = psf.tile([P, GRP * P], F32, name="f_ps")
             for a in range(GRP):
-                i = GRP * gi - NB + a
-                v_ps = psv.tile([P, D], F32, name="v_ps")
-                nc.tensor.matmul_mx(
-                    out=v_ps[:],
-                    lhsT=codes[:, a * P : (a + 1) * P].bitcast(FP8X4),
-                    lhsT_scale=scales[:, a * P : (a + 1) * P],
-                    rhs=w_codes[:].bitcast(FP8X4),
-                    rhs_scale=w_scales[:],
-                    start=True,
-                    stop=True,
+                nc.tensor.transpose(
+                    out=f_ps[c][:, a * P : (a + 1) * P],
+                    in_=nrm[g][:, a, c * P : (c + 1) * P],
+                    identity=ident_f[:],
                 )
-                for j in range(TAPS - 1, -1, -1):
-                    m = i + NB - j
-                    if 0 <= m < RUN:
-                        nc.vector.scalar_tensor_tensor(
-                            out=acc[m][:],
-                            in0=v_ps[:],
-                            scalar=a_f[:, m, j : j + 1],
-                            in1=acc[m][:],
-                            op0=ALU.mult,
-                            op1=ALU.add,
-                            accum_out=(sums[m // GRP][:, m % GRP : m % GRP + 1] if j == TAPS - 1 else None),
-                        )
-            if gi >= 1:
-                finish(gi - 1)
+
+        def affine(g, c):
+            if c == 0:
+                y_t[g] = big_pool.tile([P, GRP, GRP * P], F32, name="y_t")
+            nc.scalar.activation(
+                out=y_t[g][:, c, :],
+                in_=f_ps[c][:],
+                func=ACT.Identity,
+                scale=gb[:, c : c + 1],
+                bias=gb[:, 4 + c : 5 + c],
+            )
+
+        def to_rows(g, a):
+            b_ps[a] = psb.tile([P, D], F32, name="b_ps")
+            for c in range(GRP):
+                nc.tensor.transpose(
+                    out=b_ps[a][:, c * P : (c + 1) * P],
+                    in_=y_t[g][:, c, a * P : (a + 1) * P],
+                    identity=ident_f[:],
+                )
+
+        def leave(g, a):
+            if a == 0:
+                o_sb[g] = out_pool.tile([P, GRP, D], F32, name="o_sb")
+            nc.scalar.copy(out=o_sb[g][:, a, :], in_=b_ps[a][:])
+
+        def store(g):
+            nc.sync.dma_start(out=o_rows[:, GRP * g : GRP * (g + 1), :], in_=o_sb[g][:])
+
+        for k in range(-7, NT + 10):
+            if 0 <= k + 2 < NT:
+                project(k + 2)
+            g, r = divmod(k - 13, GRP)
+            if r == 0 and 0 <= g - 1 < NG:
+                leave(g - 1, 2)
+                leave(g - 1, 3)
+                store(g - 1)
+            if 0 <= g < NG:
+                if r == 0:
+                    to_features(g, 0)
+                    to_features(g, 1)
+                if r == 1:
+                    affine(g, 0)
+                    affine(g, 1)
+                    to_features(g, 2)
+                    to_features(g, 3)
+                if r == 2:
+                    affine(g, 2)
+                    affine(g, 3)
+                    to_rows(g, 0)
+                    to_rows(g, 1)
+                if r == 3:
+                    leave(g, 0)
+                    leave(g, 1)
+                    to_rows(g, 2)
+                    to_rows(g, 3)
+            g, r = divmod(k + 7, GRP)
+            if 0 <= g < NG_IN:
+                if r == 0:
+                    turn(g, x_srcs(g), 0)
+                if r == 1:
+                    regroup(g, 0)
+                    turn(g, x_srcs(g), 1)
+                if r == 2:
+                    regroup(g, 1)
+            if 0 <= k - 5 < RUN:
+                squares(k - 5)
+            if 0 <= k + 4 < RUN:
+                bias_part(k + 4)
+            if 0 <= k + 3 < RUN:
+                residual(k + 3)
+            g, r = divmod(k - 9, GRP)
+            if 0 <= g < NG:
+                if r == 0:
+                    stats(g)
+                normalise(GRP * g + r)
+            if 0 <= k < NT:
+                taps(k)
+            g, r = divmod(k + 4, GRP)
+            if r == 0 and 0 <= g < NG_IN:
+                codes[g] = grp_pool.tile([P, D], U32, name="codes", align_bytes=64)
+                scales[g] = grp_pool.tile([P, D], U8, name="scales", align_bytes=64)
+                quantise(g, codes[g][:], scales[g][:])

@@ -21,7 +21,8 @@ TAPS = 5
 NB = 2
 GRP = 4
 EPS = 1e-5
-CHUNK = 8
+CHUNKS = [2, 6, 8, 8, 8, 8, 8, 8, 8]
+TAIL = 8
 
 FLOPS = 2 * ROWS * D * D + 2 * ROWS * TAPS * D
 
@@ -54,13 +55,20 @@ def tile_crosssliceattention_pb_t_kernel(tc, x, Wv, bv, attn_band, gamma, beta, 
         hi_view = xf[RUN:ROWS, :].rearrange("(p t) d -> p t d", t=RUN)
         nc.sync.dma_start(out=halo[1:113, 0:NB, :], in_=lo_view[0:112, 0:NB, :])
         nc.sync.dma_start(out=halo[113:128, 0:NB, :], in_=lo_view[112:127, 0:NB, :])
-        xc = []
-        for k in range(RUN // CHUNK):
-            t = const.tile([P, CHUNK, D], BF16, name="xc%d" % k)
-            nc.sync.dma_start(out=t[:], in_=x_rows[:, k * CHUNK : (k + 1) * CHUNK, :])
-            xc.append(t)
+        x_home = {}
+        first = 0
+        for n_tiles in CHUNKS:
+            t = const.tile([P, n_tiles, D], BF16, name="xc%d" % first)
+            nc.sync.dma_start(out=t[:], in_=x_rows[:, first : first + n_tiles, :])
+            for i in range(n_tiles):
+                x_home[first + i] = t[:, i, :]
+            first += n_tiles
         nc.sync.dma_start(out=halo[0:112, NB : 2 * NB, :], in_=hi_view[0:112, 0:NB, :])
         nc.sync.dma_start(out=halo[112:127, NB : 2 * NB, :], in_=hi_view[112:127, 0:NB, :])
+        gamma_b = const.tile([P, D], BF16, name="gamma_b")
+        nc.sync.dma_start(out=gamma_b[:], in_=gamma.partition_broadcast(P))
+        beta_b = const.tile([P, D], BF16, name="beta_b")
+        nc.sync.dma_start(out=beta_b[:], in_=beta.partition_broadcast(P))
 
         a_bf = const.tile([P, RUN * TAPS], BF16, name="a_bf")
         nc.scalar.dma_start(
@@ -86,37 +94,34 @@ def tile_crosssliceattention_pb_t_kernel(tc, x, Wv, bv, attn_band, gamma, beta, 
                 return halo[:, i + NB, :]
             if i >= RUN:
                 return halo[:, i - RUN + NB, :]
-            return xc[i // CHUNK][:, i % CHUNK, :]
+            return x_home[i]
 
         a_f = const.tile([P, RUN, TAPS], F32, name="a_f")
         nc.vector.tensor_copy(out=a_f[:].rearrange("p t j -> p (t j)"), in_=a_bf[:])
         csum = const.tile([P, RUN], F32, name="csum")
         nc.vector.reduce_sum(out=csum[:], in_=a_f[:], axis=AX.X)
 
-        gps = psx.tile([P, P], BF16, name="gps", tag="xt")
-        nc.tensor.transpose(out=gps[:], in_=gbrow[:], identity=ident_b[:])
         gb = const.tile([P, 8], F32, name="gb")
-        nc.vector.tensor_copy(out=gb[:], in_=gps[:, 0:8])
 
         grouped = {}
         xt_ps = {}
 
-        def turn(key, srcs, h):
-            xt = psx.tile([P, 2, 2, P], F32, name="xt", tag="xt")
+        def turn(key, srcs, h, pool, tag):
+            xt = pool.tile([P, 2, 2, P], F32, name="xt", tag=tag)
             for a in range(2):
                 w32 = srcs[2 * h + a].bitcast(F32)
                 for u in range(2):
                     nc.tensor.transpose(
                         out=xt[:, a, u, :], in_=w32[:, u * P : (u + 1) * P], identity=ident_f[:]
                     )
-            xt_ps[key] = xt
+            xt_ps[(key, h)] = xt
 
-        def regroup(key, h):
+        def regroup(key, h, engine_copy):
             if h == 0:
                 grouped[key] = grp_pool.tile([P, GRP * D], BF16, name="grouped", align_bytes=64)
             g32 = grouped[key][:].bitcast(F32).rearrange("p (a t u) -> p a t u", a=GRP, u=2)
-            nc.scalar.copy(
-                out=g32[:, 2 * h : 2 * h + 2, :, :], in_=xt_ps[key][:].rearrange("p a u t -> p a t u")
+            engine_copy(
+                out=g32[:, 2 * h : 2 * h + 2, :, :], in_=xt_ps[(key, h)][:].rearrange("p a u t -> p a t u")
             )
 
         def quantise(key, codes, scales):
@@ -126,9 +131,9 @@ def tile_crosssliceattention_pb_t_kernel(tc, x, Wv, bv, attn_band, gamma, beta, 
         w_scales = const.tile([P, D], U8, name="w_scales", align_bytes=64)
         w_srcs = [w_raw[:, c, :] for c in range(GRP)]
         for h in range(2):
-            turn("w", w_srcs, h)
-            regroup("w", h)
-        quantise("w", w_codes[:], w_scales[:])
+            turn("w", w_srcs, h, psf, "f_ps")
+        for h in range(2):
+            regroup("w", h, nc.scalar.copy)
 
         NT = RUN + 2 * NB
         NG_IN = NT // GRP
@@ -139,6 +144,19 @@ def tile_crosssliceattention_pb_t_kernel(tc, x, Wv, bv, attn_band, gamma, beta, 
 
         codes = {}
         scales = {}
+
+        def quantise_x(g):
+            codes[g] = grp_pool.tile([P, D], U32, name="codes", align_bytes=64)
+            scales[g] = grp_pool.tile([P, D], U8, name="scales", align_bytes=64)
+            quantise(g, codes[g][:], scales[g][:])
+
+        for h in range(2):
+            turn(0, x_srcs(0), h, psb, "b_ps")
+        for h in range(2):
+            regroup(0, h, nc.vector.tensor_copy)
+        quantise("w", w_codes[:], w_scales[:])
+        quantise_x(0)
+
         v_ps = {}
         acc = {}
         sums = {}
@@ -205,7 +223,7 @@ def tile_crosssliceattention_pb_t_kernel(tc, x, Wv, bv, attn_band, gamma, beta, 
         def stats(g):
             mu[g] = stat_pool.tile([P, GRP], F32, name="mu")
             nc.gpsimd.tensor_scalar(
-                out=mu[g][:], in0=sums[g][:], scalar1=1.0 / D, scalar2=0.0, op0=ALU.mult, op1=ALU.add
+                out=mu[g][:], in0=sums[g][:], scalar1=-1.0 / D, scalar2=0.0, op0=ALU.mult, op1=ALU.add
             )
             var = stat_pool.tile([P, GRP], F32, name="var")
             nc.gpsimd.tensor_scalar(
@@ -222,7 +240,7 @@ def tile_crosssliceattention_pb_t_kernel(tc, x, Wv, bv, attn_band, gamma, beta, 
                 in0=acc[m][:],
                 scalar1=mu[g][:, a : a + 1],
                 scalar2=rstd[g][:, a : a + 1],
-                op0=ALU.subtract,
+                op0=ALU.add,
                 op1=ALU.mult,
             )
 
@@ -263,15 +281,46 @@ def tile_crosssliceattention_pb_t_kernel(tc, x, Wv, bv, attn_band, gamma, beta, 
         def store(g):
             nc.sync.dma_start(out=o_rows[:, GRP * g : GRP * (g + 1), :], in_=o_sb[g][:])
 
-        for k in range(-7, NT + 10):
+        def stats_one(m):
+            mu[m] = stat_pool.tile([P, 1], F32, name="mu1")
+            g, a = divmod(m, GRP)
+            nc.gpsimd.tensor_scalar(
+                out=mu[m][:], in0=sums[g][:, a : a + 1], scalar1=-1.0 / D, scalar2=0.0, op0=ALU.mult, op1=ALU.add
+            )
+            var = stat_pool.tile([P, 1], F32, name="var1")
+            nc.gpsimd.tensor_scalar(
+                out=var[:],
+                in0=ssq[g][:, a : a + 1],
+                scalar1=1.0 / (D * D * D),
+                scalar2=EPS,
+                op0=ALU.mult,
+                op1=ALU.add,
+            )
+            rstd[m] = stat_pool.tile([P, 1], F32, name="rstd1")
+            nc.gpsimd.tensor_tensor(out=rstd[m][:], in0=var[:], in1=mhalf[:, 0:1], op=ALU.pow)
+
+        def affine_on_vector(m):
+            cen = junk_pool.tile([P, D], F32, name="cen")
+            nc.vector.scalar_tensor_tensor(
+                out=cen[:], in0=acc[m][:], scalar=mu[m][:], in1=gamma_b[:], op0=ALU.add, op1=ALU.mult
+            )
+            o_one = out_pool.tile([P, D], F32, name="o_one")
+            nc.vector.scalar_tensor_tensor(
+                out=o_one[:], in0=cen[:], scalar=rstd[m][:], in1=beta_b[:], op0=ALU.mult, op1=ALU.add
+            )
+            nc.sync.dma_start(out=o_rows[:, m, :], in_=o_one[:])
+
+        NG_T = (RUN - TAIL) // GRP
+
+        for k in range(-4, NT + 4):
             if 0 <= k + 2 < NT:
                 project(k + 2)
             g, r = divmod(k - 13, GRP)
-            if r == 0 and 0 <= g - 1 < NG:
+            if r == 0 and 0 <= g - 1 < NG_T:
                 leave(g - 1, 2)
                 leave(g - 1, 3)
                 store(g - 1)
-            if 0 <= g < NG:
+            if 0 <= g < NG_T:
                 if r == 0:
                     to_features(g, 0)
                     to_features(g, 1)
@@ -291,14 +340,17 @@ def tile_crosssliceattention_pb_t_kernel(tc, x, Wv, bv, attn_band, gamma, beta, 
                     to_rows(g, 2)
                     to_rows(g, 3)
             g, r = divmod(k + 7, GRP)
-            if 0 <= g < NG_IN:
+            if 1 <= g < NG_IN:
                 if r == 0:
-                    turn(g, x_srcs(g), 0)
+                    turn(g, x_srcs(g), 0, psx, "xt")
                 if r == 1:
-                    regroup(g, 0)
-                    turn(g, x_srcs(g), 1)
+                    regroup(g, 0, nc.scalar.copy)
+                    turn(g, x_srcs(g), 1, psx, "xt")
                 if r == 2:
-                    regroup(g, 1)
+                    regroup(g, 1, nc.scalar.copy)
+            if k == 2:
+                gps = psb.tile([P, P], BF16, name="gps", tag="b_ps")
+                nc.tensor.transpose(out=gps[:], in_=gbrow[:], identity=ident_b[:])
             if 0 <= k - 5 < RUN:
                 squares(k - 5)
             if 0 <= k + 4 < RUN:
@@ -306,14 +358,18 @@ def tile_crosssliceattention_pb_t_kernel(tc, x, Wv, bv, attn_band, gamma, beta, 
             if 0 <= k + 3 < RUN:
                 residual(k + 3)
             g, r = divmod(k - 9, GRP)
-            if 0 <= g < NG:
+            if 0 <= g < NG_T:
                 if r == 0:
                     stats(g)
                 normalise(GRP * g + r)
+            if RUN - TAIL <= k - 6 < RUN:
+                stats_one(k - 6)
             if 0 <= k < NT:
                 taps(k)
+            if k == 2:
+                nc.vector.tensor_copy(out=gb[:], in_=gps[:, 0:8])
+            if RUN - TAIL <= k - 7 < RUN:
+                affine_on_vector(k - 7)
             g, r = divmod(k + 4, GRP)
-            if r == 0 and 0 <= g < NG_IN:
-                codes[g] = grp_pool.tile([P, D], U32, name="codes", align_bytes=64)
-                scales[g] = grp_pool.tile([P, D], U8, name="scales", align_bytes=64)
-                quantise(g, codes[g][:], scales[g][:])
+            if r == 0 and 1 <= g < NG_IN:
+                quantise_x(g)

@@ -23,6 +23,9 @@ GRP = 4
 EPS = 1e-5
 CHUNKS = [2, 6, 8, 8, 8, 8, 8, 8, 8]
 TAIL = 8
+OFF_MOD = 4
+OFF_RES = [1]
+NORM_ON_SCALAR = [2]
 
 FLOPS = 2 * ROWS * D * D + 2 * ROWS * TAPS * D
 
@@ -162,6 +165,7 @@ def tile_crosssliceattention_pb_t_kernel(tc, x, Wv, bv, attn_band, gamma, beta, 
         sums = {}
         ssq = {}
         mu = {}
+        shift = {}
         rstd = {}
         nrm = {}
         y_t = {}
@@ -182,10 +186,22 @@ def tile_crosssliceattention_pb_t_kernel(tc, x, Wv, bv, attn_band, gamma, beta, 
                 stop=True,
             )
 
+        def off_vector(m):
+            return m % OFF_MOD in OFF_RES
+
+        prod = {}
+
+        def first_tap_product(m):
+            prod[m] = junk_pool.tile([P, D], F32, name="prod")
+            nc.scalar.activation(out=prod[m][:], in_=v_ps[m][:], func=ACT.Copy, scale=a_f[:, m, 0:1])
+
+        def first_tap_add(m):
+            nc.gpsimd.tensor_tensor(out=acc[m][:], in0=acc[m][:], in1=prod[m][:], op=ALU.add)
+
         def taps(k):
             for j in range(TAPS - 1, -1, -1):
                 m = k - j
-                if 0 <= m < RUN:
+                if 0 <= m < RUN and not (j == 0 and off_vector(m)):
                     g, a = divmod(m, GRP)
                     nc.vector.scalar_tensor_tensor(
                         out=acc[m][:],
@@ -231,7 +247,19 @@ def tile_crosssliceattention_pb_t_kernel(tc, x, Wv, bv, attn_band, gamma, beta, 
             )
             rstd[g] = stat_pool.tile([P, GRP], F32, name="rstd")
             nc.gpsimd.tensor_tensor(out=rstd[g][:], in0=var[:], in1=mhalf[:], op=ALU.pow)
+            shift[g] = stat_pool.tile([P, GRP], F32, name="shift")
+            nc.gpsimd.tensor_tensor(out=shift[g][:], in0=mu[g][:], in1=rstd[g][:], op=ALU.mult)
             nrm[g] = big_pool.tile([P, GRP, D], F32, name="nrm")
+
+        def normalise_on_scalar(m):
+            g, a = divmod(m, GRP)
+            nc.scalar.activation(
+                out=nrm[g][:, a, :],
+                in_=acc[m][:],
+                func=ACT.Identity,
+                scale=rstd[g][:, a : a + 1],
+                bias=shift[g][:, a : a + 1],
+            )
 
         def normalise(m):
             g, a = divmod(m, GRP)
@@ -315,6 +343,11 @@ def tile_crosssliceattention_pb_t_kernel(tc, x, Wv, bv, attn_band, gamma, beta, 
         for k in range(-4, NT + 4):
             if 0 <= k + 2 < NT:
                 project(k + 2)
+            if 0 <= k + 1 < RUN and off_vector(k + 1):
+                first_tap_product(k + 1)
+                first_tap_add(k + 1)
+            if 0 <= k + 4 < RUN:
+                bias_part(k + 4)
             g, r = divmod(k - 13, GRP)
             if r == 0 and 0 <= g - 1 < NG_T:
                 leave(g - 1, 2)
@@ -353,15 +386,16 @@ def tile_crosssliceattention_pb_t_kernel(tc, x, Wv, bv, attn_band, gamma, beta, 
                 nc.tensor.transpose(out=gps[:], in_=gbrow[:], identity=ident_b[:])
             if 0 <= k - 5 < RUN:
                 squares(k - 5)
-            if 0 <= k + 4 < RUN:
-                bias_part(k + 4)
+            g, r = divmod(k - 9, GRP)
+            if 0 <= g < NG_T and r in NORM_ON_SCALAR:
+                normalise_on_scalar(GRP * g + r)
             if 0 <= k + 3 < RUN:
                 residual(k + 3)
-            g, r = divmod(k - 9, GRP)
             if 0 <= g < NG_T:
                 if r == 0:
                     stats(g)
-                normalise(GRP * g + r)
+                if r not in NORM_ON_SCALAR:
+                    normalise(GRP * g + r)
             if RUN - TAIL <= k - 6 < RUN:
                 stats_one(k - 6)
             if 0 <= k < NT:

@@ -21,10 +21,10 @@ TAPS = 5
 NB = 2
 GRP = 4
 EPS = 1e-5
-CHUNKS = [2, 6, 8, 8, 8, 8, 8, 8, 8]
+CHUNKS = [2,6,8,8,8,8,8,8,8]
 TAIL = 8
-OFF_MOD = 4
-OFF_RES = [1]
+OFF_RANGES = []
+EARLY = 8
 NORM_ON_SCALAR = [2]
 
 FLOPS = 2 * ROWS * D * D + 2 * ROWS * TAPS * D
@@ -39,9 +39,9 @@ def tile_crosssliceattention_pb_t_kernel(tc, x, Wv, bv, attn_band, gamma, beta, 
     with ExitStack() as ctx:
         const = ctx.enter_context(tc.tile_pool(name="const", bufs=1))
         grp_pool = ctx.enter_context(tc.tile_pool(name="grp", bufs=2))
-        acc_pool = ctx.enter_context(tc.tile_pool(name="accp", bufs=18))
+        acc_pool = ctx.enter_context(tc.tile_pool(name="accp", bufs=6))
         junk_pool = ctx.enter_context(tc.tile_pool(name="junkp", bufs=2))
-        stat_pool = ctx.enter_context(tc.tile_pool(name="statp", bufs=5))
+        stat_pool = ctx.enter_context(tc.tile_pool(name="statp", bufs=6))
         big_pool = ctx.enter_context(tc.tile_pool(name="bigp", bufs=2))
         out_pool = ctx.enter_context(tc.tile_pool(name="outp", bufs=3))
         psx = ctx.enter_context(tc.psum_pool(name="psx", bufs=1))
@@ -64,7 +64,7 @@ def tile_crosssliceattention_pb_t_kernel(tc, x, Wv, bv, attn_band, gamma, beta, 
             t = const.tile([P, n_tiles, D], BF16, name="xc%d" % first)
             nc.sync.dma_start(out=t[:], in_=x_rows[:, first : first + n_tiles, :])
             for i in range(n_tiles):
-                x_home[first + i] = t[:, i, :]
+                x_home[first + i] = (t, i)
             first += n_tiles
         nc.sync.dma_start(out=halo[0:112, NB : 2 * NB, :], in_=hi_view[0:112, 0:NB, :])
         nc.sync.dma_start(out=halo[112:127, NB : 2 * NB, :], in_=hi_view[112:127, 0:NB, :])
@@ -88,7 +88,6 @@ def tile_crosssliceattention_pb_t_kernel(tc, x, Wv, bv, attn_band, gamma, beta, 
         make_identity(nc, ident_f[:])
         ident_b = const.tile([P, P], BF16, name="ident_b")
         make_identity(nc, ident_b[:])
-
         mhalf = const.tile([P, GRP], F32, name="mhalf")
         nc.vector.memset(mhalf[:], -0.5)
 
@@ -97,13 +96,13 @@ def tile_crosssliceattention_pb_t_kernel(tc, x, Wv, bv, attn_band, gamma, beta, 
                 return halo[:, i + NB, :]
             if i >= RUN:
                 return halo[:, i - RUN + NB, :]
-            return x_home[i]
+            t, idx = x_home[i]
+            return t[:, idx, :]
 
         a_f = const.tile([P, RUN, TAPS], F32, name="a_f")
         nc.vector.tensor_copy(out=a_f[:].rearrange("p t j -> p (t j)"), in_=a_bf[:])
         csum = const.tile([P, RUN], F32, name="csum")
         nc.vector.reduce_sum(out=csum[:], in_=a_f[:], axis=AX.X)
-
         gb = const.tile([P, 8], F32, name="gb")
 
         grouped = {}
@@ -127,8 +126,8 @@ def tile_crosssliceattention_pb_t_kernel(tc, x, Wv, bv, attn_band, gamma, beta, 
                 out=g32[:, 2 * h : 2 * h + 2, :, :], in_=xt_ps[(key, h)][:].rearrange("p a u t -> p a t u")
             )
 
-        def quantise(key, codes, scales):
-            nc.vector.quantize_mx(out=codes.bitcast(FP8X4), scales=scales, in_=grouped[key][:])
+        def quantise(key, codes_ap, scales_ap):
+            nc.vector.quantize_mx(out=codes_ap.bitcast(FP8X4), scales=scales_ap, in_=grouped[key][:])
 
         w_codes = const.tile([P, D], U32, name="w_codes", align_bytes=64)
         w_scales = const.tile([P, D], U8, name="w_scales", align_bytes=64)
@@ -141,6 +140,7 @@ def tile_crosssliceattention_pb_t_kernel(tc, x, Wv, bv, attn_band, gamma, beta, 
         NT = RUN + 2 * NB
         NG_IN = NT // GRP
         NG = RUN // GRP
+        NG_T = (RUN - TAIL) // GRP
 
         def x_srcs(g):
             return [x_tile(GRP * g - NB + a) for a in range(GRP)]
@@ -161,10 +161,11 @@ def tile_crosssliceattention_pb_t_kernel(tc, x, Wv, bv, attn_band, gamma, beta, 
         quantise_x(0)
 
         v_ps = {}
-        acc = {}
+        accg = {}
         sums = {}
         ssq = {}
         mu = {}
+        var = {}
         shift = {}
         rstd = {}
         nrm = {}
@@ -172,6 +173,17 @@ def tile_crosssliceattention_pb_t_kernel(tc, x, Wv, bv, attn_band, gamma, beta, 
         o_sb = {}
         f_ps = {}
         b_ps = {}
+        prod = {}
+        prod_sum = {}
+
+        def acc(m):
+            return accg[m // GRP][:, m % GRP, :]
+
+        def row_sum(m):
+            return sums[m // GRP][:, m % GRP, 0:1]
+
+        def off_vector(m):
+            return any(lo <= m < hi for lo, hi in OFF_RANGES)
 
         def project(k):
             g, a = divmod(k, GRP)
@@ -186,76 +198,87 @@ def tile_crosssliceattention_pb_t_kernel(tc, x, Wv, bv, attn_band, gamma, beta, 
                 stop=True,
             )
 
-        def off_vector(m):
-            return m % OFF_MOD in OFF_RES
-
-        prod = {}
-
-        def first_tap_product(m):
-            prod[m] = junk_pool.tile([P, D], F32, name="prod")
-            nc.scalar.activation(out=prod[m][:], in_=v_ps[m][:], func=ACT.Copy, scale=a_f[:, m, 0:1])
-
-        def first_tap_add(m):
-            nc.gpsimd.tensor_tensor(out=acc[m][:], in0=acc[m][:], in1=prod[m][:], op=ALU.add)
-
         def taps(k):
             for j in range(TAPS - 1, -1, -1):
                 m = k - j
-                if 0 <= m < RUN and not (j == 0 and off_vector(m)):
-                    g, a = divmod(m, GRP)
+                if 0 <= m < RUN and not (j == TAPS - 1 and off_vector(m)):
+                    last = TAPS - 2 if off_vector(m) else TAPS - 1
                     nc.vector.scalar_tensor_tensor(
-                        out=acc[m][:],
+                        out=acc(m),
                         in0=v_ps[k][:],
                         scalar=a_f[:, m, j : j + 1],
-                        in1=acc[m][:],
+                        in1=acc(m),
                         op0=ALU.mult,
                         op1=ALU.add,
-                        accum_out=(sums[g][:, a : a + 1] if j == TAPS - 1 else None),
+                        accum_out=(row_sum(m) if j == last else None),
                     )
+
+        def last_tap_product(m):
+            prod[m] = junk_pool.tile([P, D], F32, name="prod")
+            prod_sum[m] = stat_pool.tile([P, 1], F32, name="prod_sum")
+            nc.scalar.activation(
+                out=prod[m][:],
+                in_=v_ps[m + TAPS - 1][:],
+                func=ACT.Copy,
+                scale=a_f[:, m, TAPS - 1 : TAPS],
+                accum_out=prod_sum[m][:],
+            )
+
+        def last_tap_add(m):
+            nc.gpsimd.tensor_tensor(out=acc(m), in0=acc(m), in1=prod[m][:], op=ALU.add)
+
+        def join_sums(m):
+            nc.scalar.activation(
+                out=row_sum(m), in_=row_sum(m), func=ACT.Identity, bias=prod_sum[m][:], scale=1.0
+            )
 
         def bias_part(m):
             g, a = divmod(m, GRP)
             if a == 0:
-                sums[g] = stat_pool.tile([P, GRP], F32, name="sums")
+                sums[g] = stat_pool.tile([P, GRP, 8], F32, name="sums")
                 ssq[g] = stat_pool.tile([P, GRP], F32, name="ssq")
-            acc[m] = acc_pool.tile([P, D], F32, name="acc")
-            nc.scalar.activation(out=acc[m][:], in_=bvb[:], func=ACT.Copy, scale=csum[:, m : m + 1])
+                accg[g] = acc_pool.tile([P, GRP, D], F32, name="accg")
+            nc.scalar.activation(out=acc(m), in_=bvb[:], func=ACT.Copy, scale=csum[:, m : m + 1])
 
-        def residual(m):
-            nc.gpsimd.tensor_tensor(out=acc[m][:], in0=acc[m][:], in1=x_tile(m), op=ALU.add)
+        def residual(m, n):
+            g, a = divmod(m, GRP)
+            t, idx = x_home[m]
+            nc.gpsimd.tensor_tensor(
+                out=accg[g][:, a : a + n, :],
+                in0=accg[g][:, a : a + n, :],
+                in1=t[:, idx : idx + n, :],
+                op=ALU.add,
+            )
 
         def squares(m):
             g, a = divmod(m, GRP)
             junk = junk_pool.tile([P, D], BF16, name="junk")
             nc.scalar.activation(
                 out=junk[:],
-                in_=acc[m][:],
+                in_=acc(m),
                 func=ACT.Square,
-                bias=sums[g][:, a : a + 1],
+                bias=row_sum(m),
                 scale=-1.0 * D,
                 accum_out=ssq[g][:, a : a + 1],
             )
 
-        def stats(g):
-            mu[g] = stat_pool.tile([P, GRP], F32, name="mu")
-            nc.gpsimd.tensor_scalar(
-                out=mu[g][:], in0=sums[g][:], scalar1=-1.0 / D, scalar2=0.0, op0=ALU.mult, op1=ALU.add
+        def moments(key, sum_ap, ssq_ap, n):
+            mu[key] = stat_pool.tile([P, n], F32, name="mu%d" % n)
+            nc.scalar.mul(out=mu[key][:], in_=sum_ap, mul=-1.0 / D)
+            var[key] = stat_pool.tile([P, n], F32, name="var%d" % n)
+            nc.scalar.activation(
+                out=var[key][:], in_=ssq_ap, func=ACT.Copy, scale=1.0 / (D * D * D), bias=EPS
             )
-            var = stat_pool.tile([P, GRP], F32, name="var")
-            nc.gpsimd.tensor_scalar(
-                out=var[:], in0=ssq[g][:], scalar1=1.0 / (D * D * D), scalar2=EPS, op0=ALU.mult, op1=ALU.add
-            )
-            rstd[g] = stat_pool.tile([P, GRP], F32, name="rstd")
-            nc.gpsimd.tensor_tensor(out=rstd[g][:], in0=var[:], in1=mhalf[:], op=ALU.pow)
-            shift[g] = stat_pool.tile([P, GRP], F32, name="shift")
-            nc.gpsimd.tensor_tensor(out=shift[g][:], in0=mu[g][:], in1=rstd[g][:], op=ALU.mult)
-            nrm[g] = big_pool.tile([P, GRP, D], F32, name="nrm")
+
+        def inverse_std(key, n):
+            rstd[key] = stat_pool.tile([P, n], F32, name="rstd%d" % n)
+            nc.gpsimd.tensor_tensor(out=rstd[key][:], in0=var[key][:], in1=mhalf[:, 0:n], op=ALU.pow)
 
         def normalise_on_scalar(m):
             g, a = divmod(m, GRP)
             nc.scalar.activation(
                 out=nrm[g][:, a, :],
-                in_=acc[m][:],
+                in_=acc(m),
                 func=ACT.Identity,
                 scale=rstd[g][:, a : a + 1],
                 bias=shift[g][:, a : a + 1],
@@ -265,7 +288,7 @@ def tile_crosssliceattention_pb_t_kernel(tc, x, Wv, bv, attn_band, gamma, beta, 
             g, a = divmod(m, GRP)
             nc.gpsimd.tensor_scalar(
                 out=nrm[g][:, a, :],
-                in0=acc[m][:],
+                in0=acc(m),
                 scalar1=mu[g][:, a : a + 1],
                 scalar2=rstd[g][:, a : a + 1],
                 op0=ALU.add,
@@ -309,45 +332,27 @@ def tile_crosssliceattention_pb_t_kernel(tc, x, Wv, bv, attn_band, gamma, beta, 
         def store(g):
             nc.sync.dma_start(out=o_rows[:, GRP * g : GRP * (g + 1), :], in_=o_sb[g][:])
 
-        def stats_one(m):
-            mu[m] = stat_pool.tile([P, 1], F32, name="mu1")
-            g, a = divmod(m, GRP)
-            nc.gpsimd.tensor_scalar(
-                out=mu[m][:], in0=sums[g][:, a : a + 1], scalar1=-1.0 / D, scalar2=0.0, op0=ALU.mult, op1=ALU.add
-            )
-            var = stat_pool.tile([P, 1], F32, name="var1")
-            nc.gpsimd.tensor_scalar(
-                out=var[:],
-                in0=ssq[g][:, a : a + 1],
-                scalar1=1.0 / (D * D * D),
-                scalar2=EPS,
-                op0=ALU.mult,
-                op1=ALU.add,
-            )
-            rstd[m] = stat_pool.tile([P, 1], F32, name="rstd1")
-            nc.gpsimd.tensor_tensor(out=rstd[m][:], in0=var[:], in1=mhalf[:, 0:1], op=ALU.pow)
-
         def affine_on_vector(m):
+            key = "t%d" % m
             cen = junk_pool.tile([P, D], F32, name="cen")
             nc.vector.scalar_tensor_tensor(
-                out=cen[:], in0=acc[m][:], scalar=mu[m][:], in1=gamma_b[:], op0=ALU.add, op1=ALU.mult
+                out=cen[:], in0=acc(m), scalar=mu[key][:], in1=gamma_b[:], op0=ALU.add, op1=ALU.mult
             )
             o_one = out_pool.tile([P, D], F32, name="o_one")
             nc.vector.scalar_tensor_tensor(
-                out=o_one[:], in0=cen[:], scalar=rstd[m][:], in1=beta_b[:], op0=ALU.mult, op1=ALU.add
+                out=o_one[:], in0=cen[:], scalar=rstd[key][:], in1=beta_b[:], op0=ALU.mult, op1=ALU.add
             )
             nc.sync.dma_start(out=o_rows[:, m, :], in_=o_one[:])
 
-        NG_T = (RUN - TAIL) // GRP
-
-        for k in range(-4, NT + 4):
+        for k in range(-4, NT + 10):
             if 0 <= k + 2 < NT:
                 project(k + 2)
-            if 0 <= k + 1 < RUN and off_vector(k + 1):
-                first_tap_product(k + 1)
-                first_tap_add(k + 1)
-            if 0 <= k + 4 < RUN:
+            if off_vector(k - 4):
+                last_tap_product(k - 4)
+            if 0 <= k + 4 < EARLY:
                 bias_part(k + 4)
+            if EARLY <= k + 8 < RUN:
+                bias_part(k + 8)
             g, r = divmod(k - 13, GRP)
             if r == 0 and 0 <= g - 1 < NG_T:
                 leave(g - 1, 2)
@@ -384,20 +389,37 @@ def tile_crosssliceattention_pb_t_kernel(tc, x, Wv, bv, attn_band, gamma, beta, 
             if k == 2:
                 gps = psb.tile([P, P], BF16, name="gps", tag="b_ps")
                 nc.tensor.transpose(out=gps[:], in_=gbrow[:], identity=ident_b[:])
-            if 0 <= k - 5 < RUN:
+            if off_vector(k - 5):
+                join_sums(k - 5)
+            if 0 <= k - 5 < RUN and not off_vector(k - 5):
                 squares(k - 5)
+            if off_vector(k - 6):
+                squares(k - 6)
             g, r = divmod(k - 9, GRP)
+            if 0 <= g < NG_T and r == 0:
+                moments(g, sums[g][:, :, 0], ssq[g][:], GRP)
+            if RUN - TAIL <= k - 6 < RUN:
+                m = k - 6
+                moments("t%d" % m, row_sum(m), ssq[m // GRP][:, m % GRP : m % GRP + 1], 1)
             if 0 <= g < NG_T and r in NORM_ON_SCALAR:
                 normalise_on_scalar(GRP * g + r)
-            if 0 <= k + 3 < RUN:
-                residual(k + 3)
+            if 0 <= k + 3 < EARLY:
+                residual(k + 3, 1)
+            if (k + 4) % GRP == 0 and EARLY <= k + 4 < RUN:
+                residual(k + 4, GRP)
+            if off_vector(k - 4):
+                last_tap_add(k - 4)
             if 0 <= g < NG_T:
                 if r == 0:
-                    stats(g)
+                    inverse_std(g, GRP)
+                    nrm[g] = big_pool.tile([P, GRP, D], F32, name="nrm")
+                    if len(NORM_ON_SCALAR) > 0:
+                        shift[g] = stat_pool.tile([P, GRP], F32, name="shift")
+                        nc.gpsimd.tensor_tensor(out=shift[g][:], in0=mu[g][:], in1=rstd[g][:], op=ALU.mult)
                 if r not in NORM_ON_SCALAR:
                     normalise(GRP * g + r)
             if RUN - TAIL <= k - 6 < RUN:
-                stats_one(k - 6)
+                inverse_std("t%d" % (k - 6), 1)
             if 0 <= k < NT:
                 taps(k)
             if k == 2:

@@ -23,9 +23,9 @@ GRP = 4
 EPS = 1e-5
 CHUNKS = [2,6,8,8,8,8,8,8,8]
 TAIL = 8
-OFF_RANGES = []
+OFF_A = [1,2]
 EARLY = 8
-NORM_ON_SCALAR = [2]
+NORM_ON_SCALAR = []
 
 FLOPS = 2 * ROWS * D * D + 2 * ROWS * TAPS * D
 
@@ -183,7 +183,7 @@ def tile_crosssliceattention_pb_t_kernel(tc, x, Wv, bv, attn_band, gamma, beta, 
             return sums[m // GRP][:, m % GRP, 0:1]
 
         def off_vector(m):
-            return any(lo <= m < hi for lo, hi in OFF_RANGES)
+            return 0 <= m < RUN - TAIL and m % GRP in OFF_A
 
         def project(k):
             g, a = divmod(k, GRP)
@@ -403,12 +403,12 @@ def tile_crosssliceattention_pb_t_kernel(tc, x, Wv, bv, attn_band, gamma, beta, 
                 moments("t%d" % m, row_sum(m), ssq[m // GRP][:, m % GRP : m % GRP + 1], 1)
             if 0 <= g < NG_T and r in NORM_ON_SCALAR:
                 normalise_on_scalar(GRP * g + r)
-            if 0 <= k + 3 < EARLY:
-                residual(k + 3, 1)
-            if (k + 4) % GRP == 0 and EARLY <= k + 4 < RUN:
-                residual(k + 4, GRP)
             if off_vector(k - 4):
                 last_tap_add(k - 4)
+            if 0 <= k + 3 < EARLY:
+                residual(k + 3, 1)
+            if k % 2 == 0 and EARLY <= k + 6 < RUN:
+                residual(k + 6, 2)
             if 0 <= g < NG_T:
                 if r == 0:
                     inverse_std(g, GRP)

from contextlib import ExitStack

import concourse.mybir as mybir
from concourse.masks import make_identity

F32 = mybir.dt.float32
BF16 = mybir.dt.bfloat16
U32 = mybir.dt.uint32
U8 = mybir.dt.uint8
I32 = mybir.dt.int32
FP8X4 = mybir.dt.float8_e4m3fn_x4
ALU = mybir.AluOpType
ACT = mybir.ActivationFunctionType
AX = mybir.AxisListType

P = 128
D = 512
ROWS = 8192
RUN = ROWS // P
TAPS = 5
NB = 2
GRP = 4
EPS = 1e-5
CHUNKS = [2,6,8,8,8,8,8,8,8]
TAIL = 8
OFF_A = [1,2]
EARLY = 8
NORM_ON_SCALAR = []

FLOPS = 2 * ROWS * D * D + 2 * ROWS * TAPS * D


def tile_crosssliceattention_pb_t_kernel(tc, x, Wv, bv, attn_band, gamma, beta, out):
    nc = tc.nc
    xf = x.flatten_outer_dims()
    x_rows = xf.rearrange("(p t) d -> p t d", t=RUN)
    o_rows = out.flatten_outer_dims().rearrange("(p t) d -> p t d", t=RUN)

    with ExitStack() as ctx:
        const = ctx.enter_context(tc.tile_pool(name="const", bufs=1))
        grp_pool = ctx.enter_context(tc.tile_pool(name="grp", bufs=2))
        acc_pool = ctx.enter_context(tc.tile_pool(name="accp", bufs=6))
        junk_pool = ctx.enter_context(tc.tile_pool(name="junkp", bufs=2))
        stat_pool = ctx.enter_context(tc.tile_pool(name="statp", bufs=6))
        big_pool = ctx.enter_context(tc.tile_pool(name="bigp", bufs=2))
        out_pool = ctx.enter_context(tc.tile_pool(name="outp", bufs=3))
        psx = ctx.enter_context(tc.psum_pool(name="psx", bufs=1))
        psv = ctx.enter_context(tc.psum_pool(name="psv", bufs=3))
        psf = ctx.enter_context(tc.psum_pool(name="psf", bufs=2))
        psb = ctx.enter_context(tc.psum_pool(name="psb", bufs=2))
        ctx.enter_context(tc.manual_schedule())

        w_raw = const.tile([P, GRP, D], BF16, name="w_raw")
        nc.sync.dma_start(out=w_raw[:], in_=Wv.rearrange("(c p) k -> p c k", p=P))
        halo = const.tile([P, 2 * NB, D], BF16, name="halo")
        nc.vector.memset(halo[:].bitcast(I32), 0)
        lo_view = xf[RUN - NB : RUN - NB + RUN * (P - 1), :].rearrange("(p t) d -> p t d", t=RUN)
        hi_view = xf[RUN:ROWS, :].rearrange("(p t) d -> p t d", t=RUN)
        nc.sync.dma_start(out=halo[1:113, 0:NB, :], in_=lo_view[0:112, 0:NB, :])
        nc.sync.dma_start(out=halo[113:128, 0:NB, :], in_=lo_view[112:127, 0:NB, :])
        x_home = {}
        first = 0
        for n_tiles in CHUNKS:
            t = const.tile([P, n_tiles, D], BF16, name="xc%d" % first)
            nc.sync.dma_start(out=t[:], in_=x_rows[:, first : first + n_tiles, :])
            for i in range(n_tiles):
                x_home[first + i] = (t, i)
            first += n_tiles
        nc.sync.dma_start(out=halo[0:112, NB : 2 * NB, :], in_=hi_view[0:112, 0:NB, :])
        nc.sync.dma_start(out=halo[112:127, NB : 2 * NB, :], in_=hi_view[112:127, 0:NB, :])
        gamma_b = const.tile([P, D], BF16, name="gamma_b")
        nc.sync.dma_start(out=gamma_b[:], in_=gamma.partition_broadcast(P))
        beta_b = const.tile([P, D], BF16, name="beta_b")
        nc.sync.dma_start(out=beta_b[:], in_=beta.partition_broadcast(P))

        a_bf = const.tile([P, RUN * TAPS], BF16, name="a_bf")
        nc.scalar.dma_start(
            out=a_bf[:], in_=attn_band.flatten_outer_dims().rearrange("(p t) j -> p (t j)", t=RUN)
        )
        bvb = const.tile([P, D], BF16, name="bvb")
        nc.scalar.dma_start(out=bvb[:], in_=bv.partition_broadcast(P))
        gbrow = const.tile([P, P], BF16, name="gbrow")
        nc.vector.memset(gbrow[:], 0.0)
        nc.scalar.dma_start(out=gbrow[0:4, :], in_=gamma.rearrange("(c p) -> c p", p=P))
        nc.scalar.dma_start(out=gbrow[4:8, :], in_=beta.rearrange("(c p) -> c p", p=P))

        ident_f = const.tile([P, P], F32, name="ident_f")
        make_identity(nc, ident_f[:])
        ident_b = const.tile([P, P], BF16, name="ident_b")
        make_identity(nc, ident_b[:])
        mhalf = const.tile([P, GRP], F32, name="mhalf")
        nc.vector.memset(mhalf[:], -0.5)

        def x_tile(i):
            if i < 0:
                return halo[:, i + NB, :]
            if i >= RUN:
                return halo[:, i - RUN + NB, :]
            t, idx = x_home[i]
            return t[:, idx, :]

        a_f = const.tile([P, RUN, TAPS], F32, name="a_f")
        nc.vector.tensor_copy(out=a_f[:].rearrange("p t j -> p (t j)"), in_=a_bf[:])
        csum = const.tile([P, RUN], F32, name="csum")
        nc.vector.reduce_sum(out=csum[:], in_=a_f[:], axis=AX.X)
        gb = const.tile([P, 8], F32, name="gb")

        grouped = {}
        xt_ps = {}

        def turn(key, srcs, h, pool, tag):
            xt = pool.tile([P, 2, 2, P], F32, name="xt", tag=tag)
            for a in range(2):
                w32 = srcs[2 * h + a].bitcast(F32)
                for u in range(2):
                    nc.tensor.transpose(
                        out=xt[:, a, u, :], in_=w32[:, u * P : (u + 1) * P], identity=ident_f[:]
                    )
            xt_ps[(key, h)] = xt

        def regroup(key, h, engine_copy):
            if h == 0:
                grouped[key] = grp_pool.tile([P, GRP * D], BF16, name="grouped", align_bytes=64)
            g32 = grouped[key][:].bitcast(F32).rearrange("p (a t u) -> p a t u", a=GRP, u=2)
            engine_copy(
                out=g32[:, 2 * h : 2 * h + 2, :, :], in_=xt_ps[(key, h)][:].rearrange("p a u t -> p a t u")
            )

        def quantise(key, codes_ap, scales_ap):
            nc.vector.quantize_mx(out=codes_ap.bitcast(FP8X4), scales=scales_ap, in_=grouped[key][:])

        w_codes = const.tile([P, D], U32, name="w_codes", align_bytes=64)
        w_scales = const.tile([P, D], U8, name="w_scales", align_bytes=64)
        w_srcs = [w_raw[:, c, :] for c in range(GRP)]
        for h in range(2):
            turn("w", w_srcs, h, psf, "f_ps")
        for h in range(2):
            regroup("w", h, nc.scalar.copy)

        NT = RUN + 2 * NB
        NG_IN = NT // GRP
        NG = RUN // GRP
        NG_T = (RUN - TAIL) // GRP

        def x_srcs(g):
            return [x_tile(GRP * g - NB + a) for a in range(GRP)]

        codes = {}
        scales = {}

        def quantise_x(g):
            codes[g] = grp_pool.tile([P, D], U32, name="codes", align_bytes=64)
            scales[g] = grp_pool.tile([P, D], U8, name="scales", align_bytes=64)
            quantise(g, codes[g][:], scales[g][:])

        for h in range(2):
            turn(0, x_srcs(0), h, psb, "b_ps")
        for h in range(2):
            regroup(0, h, nc.vector.tensor_copy)
        quantise("w", w_codes[:], w_scales[:])
        quantise_x(0)

        v_ps = {}
        accg = {}
        sums = {}
        ssq = {}
        mu = {}
        var = {}
        shift = {}
        rstd = {}
        nrm = {}
        y_t = {}
        o_sb = {}
        f_ps = {}
        b_ps = {}
        prod = {}
        prod_sum = {}

        def acc(m):
            return accg[m // GRP][:, m % GRP, :]

        def row_sum(m):
            return sums[m // GRP][:, m % GRP, 0:1]

        def off_vector(m):
            return 0 <= m < RUN - TAIL and m % GRP in OFF_A

        def project(k):
            g, a = divmod(k, GRP)
            v_ps[k] = psv.tile([P, D], F32, name="v_ps")
            nc.tensor.matmul_mx(
                out=v_ps[k][:],
                lhsT=codes[g][:, a * P : (a + 1) * P].bitcast(FP8X4),
                lhsT_scale=scales[g][:, a * P : (a + 1) * P],
                rhs=w_codes[:].bitcast(FP8X4),
                rhs_scale=w_scales[:],
                start=True,
                stop=True,
            )

        def taps(k):
            for j in range(TAPS - 1, -1, -1):
                m = k - j
                if 0 <= m < RUN and not (j == TAPS - 1 and off_vector(m)):
                    last = TAPS - 2 if off_vector(m) else TAPS - 1
                    nc.vector.scalar_tensor_tensor(
                        out=acc(m),
                        in0=v_ps[k][:],
                        scalar=a_f[:, m, j : j + 1],
                        in1=acc(m),
                        op0=ALU.mult,
                        op1=ALU.add,
                        accum_out=(row_sum(m) if j == last else None),
                    )

        def last_tap_product(m):
            prod[m] = junk_pool.tile([P, D], F32, name="prod")
            prod_sum[m] = stat_pool.tile([P, 1], F32, name="prod_sum")
            nc.scalar.activation(
                out=prod[m][:],
                in_=v_ps[m + TAPS - 1][:],
                func=ACT.Copy,
                scale=a_f[:, m, TAPS - 1 : TAPS],
                accum_out=prod_sum[m][:],
            )

        def last_tap_add(m):
            nc.gpsimd.tensor_tensor(out=acc(m), in0=acc(m), in1=prod[m][:], op=ALU.add)

        def join_sums(m):
            nc.scalar.activation(
                out=row_sum(m), in_=row_sum(m), func=ACT.Identity, bias=prod_sum[m][:], scale=1.0
            )

        def bias_part(m):
            g, a = divmod(m, GRP)
            if a == 0:
                sums[g] = stat_pool.tile([P, GRP, 8], F32, name="sums")
                ssq[g] = stat_pool.tile([P, GRP], F32, name="ssq")
                accg[g] = acc_pool.tile([P, GRP, D], F32, name="accg")
            nc.scalar.activation(out=acc(m), in_=bvb[:], func=ACT.Copy, scale=csum[:, m : m + 1])

        def residual(m, n):
            g, a = divmod(m, GRP)
            t, idx = x_home[m]
            nc.gpsimd.tensor_tensor(
                out=accg[g][:, a : a + n, :],
                in0=accg[g][:, a : a + n, :],
                in1=t[:, idx : idx + n, :],
                op=ALU.add,
            )

        def squares(m):
            g, a = divmod(m, GRP)
            junk = junk_pool.tile([P, D], BF16, name="junk")
            nc.scalar.activation(
                out=junk[:],
                in_=acc(m),
                func=ACT.Square,
                bias=row_sum(m),
                scale=-1.0 * D,
                accum_out=ssq[g][:, a : a + 1],
            )

        def moments(key, sum_ap, ssq_ap, n):
            mu[key] = stat_pool.tile([P, n], F32, name="mu%d" % n)
            nc.scalar.mul(out=mu[key][:], in_=sum_ap, mul=-1.0 / D)
            var[key] = stat_pool.tile([P, n], F32, name="var%d" % n)
            nc.scalar.activation(
                out=var[key][:], in_=ssq_ap, func=ACT.Copy, scale=1.0 / (D * D * D), bias=EPS
            )

        def inverse_std(key, n):
            rstd[key] = stat_pool.tile([P, n], F32, name="rstd%d" % n)
            nc.gpsimd.tensor_tensor(out=rstd[key][:], in0=var[key][:], in1=mhalf[:, 0:n], op=ALU.pow)

        def normalise_on_scalar(m):
            g, a = divmod(m, GRP)
            nc.scalar.activation(
                out=nrm[g][:, a, :],
                in_=acc(m),
                func=ACT.Identity,
                scale=rstd[g][:, a : a + 1],
                bias=shift[g][:, a : a + 1],
            )

        def normalise(m):
            g, a = divmod(m, GRP)
            nc.gpsimd.tensor_scalar(
                out=nrm[g][:, a, :],
                in0=acc(m),
                scalar1=mu[g][:, a : a + 1],
                scalar2=rstd[g][:, a : a + 1],
                op0=ALU.add,
                op1=ALU.mult,
            )

        def to_features(g, c):
            f_ps[c] = psf.tile([P, GRP * P], F32, name="f_ps")
            for a in range(GRP):
                nc.tensor.transpose(
                    out=f_ps[c][:, a * P : (a + 1) * P],
                    in_=nrm[g][:, a, c * P : (c + 1) * P],
                    identity=ident_f[:],
                )

        def affine(g, c):
            if c == 0:
                y_t[g] = big_pool.tile([P, GRP, GRP * P], F32, name="y_t")
            nc.scalar.activation(
                out=y_t[g][:, c, :],
                in_=f_ps[c][:],
                func=ACT.Identity,
                scale=gb[:, c : c + 1],
                bias=gb[:, 4 + c : 5 + c],
            )

        def to_rows(g, a):
            b_ps[a] = psb.tile([P, D], F32, name="b_ps")
            for c in range(GRP):
                nc.tensor.transpose(
                    out=b_ps[a][:, c * P : (c + 1) * P],
                    in_=y_t[g][:, c, a * P : (a + 1) * P],
                    identity=ident_f[:],
                )

        def leave(g, a):
            if a == 0:
                o_sb[g] = out_pool.tile([P, GRP, D], F32, name="o_sb")
            nc.scalar.copy(out=o_sb[g][:, a, :], in_=b_ps[a][:])

        def store(g):
            nc.sync.dma_start(out=o_rows[:, GRP * g : GRP * (g + 1), :], in_=o_sb[g][:])

        def affine_on_vector(m):
            key = "t%d" % m
            cen = junk_pool.tile([P, D], F32, name="cen")
            nc.vector.scalar_tensor_tensor(
                out=cen[:], in0=acc(m), scalar=mu[key][:], in1=gamma_b[:], op0=ALU.add, op1=ALU.mult
            )
            o_one = out_pool.tile([P, D], F32, name="o_one")
            nc.vector.scalar_tensor_tensor(
                out=o_one[:], in0=cen[:], scalar=rstd[key][:], in1=beta_b[:], op0=ALU.mult, op1=ALU.add
            )
            nc.sync.dma_start(out=o_rows[:, m, :], in_=o_one[:])

        for k in range(-4, NT + 10):
            if 0 <= k + 2 < NT:
                project(k + 2)
            if off_vector(k - 4):
                last_tap_product(k - 4)
            if 0 <= k + 4 < EARLY:
                bias_part(k + 4)
            if EARLY <= k + 8 < RUN:
                bias_part(k + 8)
            g, r = divmod(k - 13, GRP)
            if r == 0 and 0 <= g - 1 < NG_T:
                leave(g - 1, 2)
                leave(g - 1, 3)
                store(g - 1)
            if 0 <= g < NG_T:
                if r == 0:
                    to_features(g, 0)
                    to_features(g, 1)
                if r == 1:
                    affine(g, 0)
                    affine(g, 1)
                    to_features(g, 2)
                    to_features(g, 3)
                if r == 2:
                    affine(g, 2)
                    affine(g, 3)
                    to_rows(g, 0)
                    to_rows(g, 1)
                if r == 3:
                    leave(g, 0)
                    leave(g, 1)
                    to_rows(g, 2)
                    to_rows(g, 3)
            g, r = divmod(k + 7, GRP)
            if 1 <= g < NG_IN:
                if r == 0:
                    turn(g, x_srcs(g), 0, psx, "xt")
                if r == 1:
                    regroup(g, 0, nc.scalar.copy)
                    turn(g, x_srcs(g), 1, psx, "xt")
                if r == 2:
                    regroup(g, 1, nc.scalar.copy)
            if k == 2:
                gps = psb.tile([P, P], BF16, name="gps", tag="b_ps")
                nc.tensor.transpose(out=gps[:], in_=gbrow[:], identity=ident_b[:])
            if off_vector(k - 5):
                join_sums(k - 5)
            if 0 <= k - 5 < RUN and not off_vector(k - 5):
                squares(k - 5)
            if off_vector(k - 6):
                squares(k - 6)
            g, r = divmod(k - 9, GRP)
            if 0 <= g < NG_T and r == 0:
                moments(g, sums[g][:, :, 0], ssq[g][:], GRP)
            if RUN - TAIL <= k - 6 < RUN:
                m = k - 6
                moments("t%d" % m, row_sum(m), ssq[m // GRP][:, m % GRP : m % GRP + 1], 1)
            if 0 <= g < NG_T and r in NORM_ON_SCALAR:
                normalise_on_scalar(GRP * g + r)
            if off_vector(k - 4):
                last_tap_add(k - 4)
            if 0 <= k + 3 < EARLY:
                residual(k + 3, 1)
            if k % 2 == 0 and EARLY <= k + 6 < RUN:
                residual(k + 6, 2)
            if 0 <= g < NG_T:
                if r == 0:
                    inverse_std(g, GRP)
                    nrm[g] = big_pool.tile([P, GRP, D], F32, name="nrm")
                    if len(NORM_ON_SCALAR) > 0:
                        shift[g] = stat_pool.tile([P, GRP], F32, name="shift")
                        nc.gpsimd.tensor_tensor(out=shift[g][:], in0=mu[g][:], in1=rstd[g][:], op=ALU.mult)
                if r not in NORM_ON_SCALAR:
                    normalise(GRP * g + r)
            if RUN - TAIL <= k - 6 < RUN:
                inverse_std("t%d" % (k - 6), 1)
            if 0 <= k < NT:
                taps(k)
            if k == 2:
                nc.vector.tensor_copy(out=gb[:], in_=gps[:, 0:8])
            if RUN - TAIL <= k - 7 < RUN:
                affine_on_vector(k - 7)
            g, r = divmod(k + 4, GRP)
            if r == 0 and 1 <= g < NG_IN:
                quantise_x(g)
